import numpy as np
import ml_dtypes


def mxq(x, axis, fmt="e4m3"):
    dtype, down = {"e4m3": (ml_dtypes.float8_e4m3fn, 7), "e5m2": (ml_dtypes.float8_e5m2, 14)}[fmt]
    v = np.moveaxis(np.asarray(x, np.float32).astype(ml_dtypes.bfloat16).astype(np.float64), axis, -1)
    blocks = v.reshape(v.shape[:-1] + (-1, 32))
    amax = np.abs(blocks).max(-1, keepdims=True)
    byte = np.maximum(np.where(amax > 0, np.frexp(amax)[1] - 1 + 127, 0) - down, 1)
    scale = np.exp2(byte - 127.0)
    codes = (blocks / scale).astype(np.float32).astype(dtype).astype(np.float64)
    return np.moveaxis((codes * scale).reshape(v.shape), -1, axis)


WIDE = False


def mx_kscale(k):
    if not WIDE:
        return np.ones(k)
    levels = np.array([10, -10, 5, -5, 0])
    a = np.random.permutation(np.resize(levels, k // 512 * 4)).reshape(k // 512, 4)
    idx = np.arange(k)
    return np.exp2(a[idx // 512, idx % 128 // 32])


BF16 = ml_dtypes.bfloat16


def bf(x):
    return np.asarray(x, np.float32).astype(BF16)


def f64(x):
    return np.asarray(x).astype(np.float64)


B, C, HH, WW, NH, HD, F = 4, 512, 16, 16, 8, 64, 2048
E = NH * HD


def setup_inputs():
    s, t = mx_kscale(E), mx_kscale(C)
    return {"o": bf(np.random.standard_normal((B, HH, WW, E)) * 0.6 * s),
            "xn": bf(np.random.standard_normal((B, HH, WW, C)) * 0.5 * t),
            "W_O": bf(np.random.standard_normal((E, C)) / np.sqrt(E) / s[:, None] * t),
            "scale_attn": bf(0.5 * (1.0 + 0.1 * np.random.standard_normal(1))),
            "ffn1_w": bf(np.random.standard_normal((F, C)) * 3.0 / np.sqrt(C) / t),
            "ffn1_b": bf(np.random.standard_normal(F) * 0.3),
            "scale_ffn": bf(0.1 * (1.0 + 0.1 * np.random.standard_normal(1)))}


def reference(o, xn, W_O, scale_attn, ffn1_w, ffn1_b, scale_ffn):
    p = (mxq(f64(o), 3, "e4m3") @ mxq(f64(W_O), 0, "e4m3")) * f64(scale_attn)
    y = np.maximum(f64(xn) + p, 0.0)
    u = (mxq(y, 3, "e4m3") @ mxq(f64(ffn1_w), 1, "e4m3").T) + f64(ffn1_b)
    return np.maximum(u * f64(scale_ffn), 0.0)

@@ -1,0 +1,230 @@
+from contextlib import ExitStack
+
+import concourse.masks as masks
+import concourse.mybir as mybir
+
+F32 = mybir.dt.float32
+BF16 = mybir.dt.bfloat16
+U32 = mybir.dt.uint32
+U8 = mybir.dt.uint8
+FP8X4 = mybir.dt.float8_e4m3fn_x4
+ALU = mybir.AluOpType
+ACT = mybir.ActivationFunctionType
+
+P = 128
+PACK = 4
+TOKENS = 4 * 16 * 16
+K = 512
+F = 2048
+TILES = TOKENS // P
+HALF = TILES // 2
+CHUNK = 512
+CHUNKS = F // CHUNK
+ROWS = CHUNK // P
+LEAD = 2
+
+FLOPS = 2 * TOKENS * K * K + 2 * TOKENS * K * F
+
+
+def tile_transformerconvblock_pb_kernel(
+    tc, o, xn, W_O, scale_attn, ffn1_w, ffn1_b, scale_ffn, out
+):
+    nc = tc.nc
+    with ExitStack() as ctx:
+        keep = ctx.enter_context(tc.tile_pool(name="keep", bufs=1))
+        results = ctx.enter_context(tc.tile_pool(name="results", bufs=3))
+        psum_words = ctx.enter_context(tc.psum_pool(name="psum_words", bufs=2))
+        psum_z = ctx.enter_context(tc.psum_pool(name="psum_z", bufs=2))
+        psum_p = ctx.enter_context(tc.psum_pool(name="psum_p", bufs=1))
+        psum_u = ctx.enter_context(tc.psum_pool(name="psum_u", bufs=3))
+
+        o_dram = o.rearrange("b h w e -> (b h w) e").rearrange("(p i) e -> p i e", i=TILES)
+        xn_dram = xn.rearrange("b h w c -> (b h w) c").rearrange("(p i) c -> p i c", i=TILES)
+        out_dram = out.rearrange("b h w f -> (b h w) f").rearrange("(p i) f -> p i f", i=TILES)
+        w_dram = ffn1_w.rearrange("(n j r) c -> j n r c", n=CHUNKS, r=ROWS)
+        wo_dram = W_O.rearrange("(u q e) c -> q u e c", u=2, e=2)
+
+        ident_f32 = keep.tile([P, P], F32)
+        masks.make_identity(nc, ident_f32[:])
+        ident_bf16 = keep.tile([P, P], BF16)
+        masks.make_identity(nc, ident_bf16[:])
+        ones = keep.tile([P, P], BF16)
+        nc.vector.memset(ones[:], 1.0)
+        bias_row = keep.tile([P, F], BF16)
+        nc.vector.memset(bias_row[:], 0.0)
+        attn_bf16 = keep.tile([P, 1], BF16)
+        ffn_bf16 = keep.tile([P, 1], BF16)
+        with nc.allow_non_contiguous_dma(reason="one bfloat16 scalar to every partition"):
+            nc.scalar.dma_start(out=attn_bf16[:], in_=scale_attn.partition_broadcast(P))
+            nc.scalar.dma_start(out=ffn_bf16[:], in_=scale_ffn.partition_broadcast(P))
+        nc.scalar.dma_start(out=bias_row[0:1, :], in_=ffn1_b.rearrange("(a f) -> a f", a=1))
+        attn = keep.tile([P, 1], F32)
+        nc.vector.tensor_copy(out=attn[:], in_=attn_bf16[:])
+        ffn = keep.tile([P, 1], F32)
+        nc.vector.tensor_copy(out=ffn[:], in_=ffn_bf16[:])
+
+        wo_raw = keep.tile([P, PACK * K], BF16)
+        o_sb = keep.tile([P, TILES * K], BF16)
+        xn_sb = keep.tile([P, TILES * K], BF16)
+        w_sb = keep.tile([P, CHUNKS * ROWS * K], BF16)
+        o_tiles = o_sb[:].rearrange("p (i e) -> p i e", i=TILES)
+        xn_tiles = xn_sb[:].rearrange("p (i c) -> p i c", i=TILES)
+        w_chunks = w_sb[:].rearrange("j (n r c) -> j n r c", n=CHUNKS, r=ROWS)
+        first = slice(0, HALF)
+        second = slice(HALF, TILES)
+        nc.sync.dma_start(out=wo_raw[:].rearrange("q (u e c) -> q u e c", u=2, e=2), in_=wo_dram)
+        nc.sync.dma_start(out=o_tiles[:, first, :], in_=o_dram[:, first, :])
+        nc.sync.dma_start(out=xn_tiles[:, first, :], in_=xn_dram[:, first, :])
+        for n in range(CHUNKS):
+            nc.sync.dma_start(out=w_chunks[:, n], in_=w_dram[:, n])
+        nc.sync.dma_start(out=o_tiles[:, second, :], in_=o_dram[:, second, :])
+        nc.sync.dma_start(out=xn_tiles[:, second, :], in_=xn_dram[:, second, :])
+
+        wo_grouped = keep.tile([P, K * PACK], BF16, align_bytes=64)
+        wo_codes = keep.tile([P, K], U32, align_bytes=64)
+        wo_scales = keep.tile([P, K], U8, align_bytes=64)
+        o_grouped = keep.tile([P, TOKENS * PACK], BF16, align_bytes=64)
+        o_codes = keep.tile([P, TOKENS], U32, align_bytes=64)
+        o_scales = keep.tile([P, TOKENS], U8, align_bytes=64)
+        w_grouped = keep.tile([P, F * PACK], BF16, align_bytes=64)
+        w_codes = keep.tile([P, F], U32, align_bytes=64)
+        w_scales = keep.tile([P, F], U8, align_bytes=64)
+        y_grouped = keep.tile([P, TOKENS * PACK], BF16, align_bytes=64)
+        y_codes = keep.tile([P, TOKENS], U32, align_bytes=64)
+        y_scales = keep.tile([P, TOKENS], U8, align_bytes=64)
+        z_sb = keep.tile([P, TILES * K], BF16)
+        bias_all = keep.tile([P, F], F32)
+
+        def quantise(grouped, codes, scales, start, count):
+            nc.vector.quantize_mx(
+                out=codes[:, start : start + count].bitcast(FP8X4),
+                scales=scales[:, start : start + count],
+                in_=grouped[:, PACK * start : PACK * (start + count)],
+            )
+
+        nc.vector.tensor_copy(
+            out=wo_grouped[:].rearrange("q (c t) -> q c t", t=PACK),
+            in_=wo_raw[:].rearrange("q (t c) -> q c t", t=PACK),
+        )
+        quantise(wo_grouped, wo_codes, wo_scales, 0, K)
+
+        o_words = o_sb[:].bitcast(F32).rearrange("p (i u q) -> p i u q", i=TILES, u=2)
+        o_grouped_words = o_grouped[:].bitcast(F32).rearrange("q (i p u) -> q i p u", i=TILES, u=2)
+        w_words = w_sb[:].bitcast(F32).rearrange(
+            "j (n r u q) -> j n r u q", n=CHUNKS, r=ROWS, u=2
+        )
+        w_grouped_words = w_grouped[:].bitcast(F32).rearrange(
+            "q (n j r u) -> q n j r u", n=CHUNKS, r=ROWS, u=2
+        )
+
+        def prepare_o(half):
+            for i in range(half * HALF, (half + 1) * HALF, 2):
+                bank = psum_words.tile([P, 2, 2, P], F32, tag="words")
+                for a in range(2):
+                    for u in range(2):
+                        nc.tensor.transpose(bank[:, a, u, :], o_words[:, i + a, u, :], ident_f32[:])
+                nc.scalar.copy(
+                    out=o_grouped_words[:, i : i + 2, :, :],
+                    in_=bank[:].rearrange("q a u p -> q a p u"),
+                )
+            quantise(o_grouped, o_codes, o_scales, half * HALF * P, HALF * P)
+
+        def prepare_w(n):
+            for r in range(0, ROWS, 2):
+                bank = psum_words.tile([P, 2, 2, P], F32, tag="words")
+                for a in range(2):
+                    for u in range(2):
+                        nc.tensor.transpose(bank[:, a, u, :], w_words[:, n, r + a, u, :], ident_f32[:])
+                nc.scalar.copy(
+                    out=w_grouped_words[:, n, :, r : r + 2, :],
+                    in_=bank[:].rearrange("q a u j -> q j a u"),
+                )
+            quantise(w_grouped, w_codes, w_scales, n * CHUNK, CHUNK)
+
+        def spread_bias():
+            for n in range(CHUNKS):
+                cols = slice(n * CHUNK, (n + 1) * CHUNK)
+                bank = psum_u.tile([P, CHUNK], F32, tag="u")
+                nc.tensor.matmul(out=bank[:], lhsT=ones[:], rhs=bias_row[:, cols], start=True, stop=True)
+                nc.scalar.copy(out=bias_all[:, cols], in_=bank[:])
+
+        z_pairs = z_sb[:].rearrange("p (i u q e) -> p i u q e", i=TILES, u=2, e=2)
+        y_grouped_tiles = y_grouped[:].rearrange("q (i p t) -> q i p t", i=TILES, t=PACK)
+
+        def first_matmul(i):
+            tokens = slice(i * P, (i + 1) * P)
+            cols = slice(i * K, (i + 1) * K)
+            p_bank = psum_p.tile([P, K], F32, tag="p")
+            nc.tensor.matmul_mx(
+                out=p_bank[:],
+                lhsT=o_codes[:, tokens].bitcast(FP8X4),
+                lhsT_scale=o_scales[:, tokens],
+                rhs=wo_codes[:].bitcast(FP8X4),
+                rhs_scale=wo_scales[:],
+                start=True,
+                stop=True,
+            )
+            nc.vector.scalar_tensor_tensor(
+                out=z_sb[:, cols],
+                in0=p_bank[:],
+                scalar=attn[:, 0:1],
+                in1=xn_sb[:, cols],
+                op0=ALU.mult,
+                op1=ALU.add,
+            )
+            z_bank = psum_z.tile([P, PACK, P], BF16, tag="z")
+            for u in range(2):
+                for e in range(2):
+                    nc.tensor.transpose(z_bank[:, 2 * u + e, :], z_pairs[:, i, u, :, e], ident_bf16[:])
+            nc.scalar.activation(
+                out=y_grouped_tiles[:, i, :, :],
+                in_=z_bank[:].rearrange("q t p -> q p t"),
+                func=ACT.Relu,
+            )
+            quantise(y_grouped, y_codes, y_scales, i * P, P)
+
+        def second_matmul(i):
+            tokens = slice(i * P, (i + 1) * P)
+            h_tile = results.tile([P, F], F32, tag="h")
+            for n in range(CHUNKS):
+                cols = slice(n * CHUNK, (n + 1) * CHUNK)
+                u_bank = psum_u.tile([P, CHUNK], F32, tag="u")
+                nc.tensor.matmul_mx(
+                    out=u_bank[:],
+                    lhsT=y_codes[:, tokens].bitcast(FP8X4),
+                    lhsT_scale=y_scales[:, tokens],
+                    rhs=w_codes[:, cols].bitcast(FP8X4),
+                    rhs_scale=w_scales[:, cols],
+                    start=True,
+                    stop=True,
+                )
+                nc.vector.tensor_tensor(
+                    out=h_tile[:, cols], in0=u_bank[:], in1=bias_all[:, cols], op=ALU.add
+                )
+                if n % 2 == 0:
+                    nc.scalar.activation(
+                        out=h_tile[:, cols], in_=h_tile[:, cols], func=ACT.Relu, scale=ffn[:, 0:1]
+                    )
+                else:
+                    nc.gpsimd.tensor_scalar(
+                        out=h_tile[:, cols],
+                        in0=h_tile[:, cols],
+                        scalar1=ffn[:, 0:1],
+                        scalar2=0.0,
+                        op0=ALU.mult,
+                        op1=ALU.max,
+                    )
+            nc.sync.dma_start(out=out_dram[:, i, :], in_=h_tile[:])
+
+        prepare_o(0)
+        for i in range(LEAD):
+            first_matmul(i)
+        spread_bias()
+        for n in range(CHUNKS):
+            prepare_w(n)
+        for i in range(LEAD, TILES + LEAD):
+            if i == HALF:
+                prepare_o(1)
+            if i < TILES:
+                first_matmul(i)
+            second_matmul(i - LEAD)

@@ -21,7 +21,11 @@ HALF = TILES // 2
 CHUNK = 512
 CHUNKS = F // CHUNK
 ROWS = CHUNK // P
-LEAD = 2
+PAIRS = TILES // 2
+ROUND = 2 * CHUNKS
+BANKS = PAIRS * ROUND
+W_BANKS = 2 * CHUNKS
+AHEAD = 2
 
 FLOPS = 2 * TOKENS * K * K + 2 * TOKENS * K * F
 
@@ -31,12 +35,12 @@ def tile_transformerconvblock_pb_kernel(
 ):
     nc = tc.nc
     with ExitStack() as ctx:
+        ctx.enter_context(tc.manual_schedule())
         keep = ctx.enter_context(tc.tile_pool(name="keep", bufs=1))
-        results = ctx.enter_context(tc.tile_pool(name="results", bufs=3))
+        results = ctx.enter_context(tc.tile_pool(name="results", bufs=12))
         psum_words = ctx.enter_context(tc.psum_pool(name="psum_words", bufs=2))
-        psum_z = ctx.enter_context(tc.psum_pool(name="psum_z", bufs=2))
-        psum_p = ctx.enter_context(tc.psum_pool(name="psum_p", bufs=1))
-        psum_u = ctx.enter_context(tc.psum_pool(name="psum_u", bufs=3))
+        psum_first = ctx.enter_context(tc.psum_pool(name="psum_first", bufs=3))
+        psum_u = ctx.enter_context(tc.psum_pool(name="psum_u", bufs=AHEAD + 1))
 
         o_dram = o.rearrange("b h w e -> (b h w) e").rearrange("(p i) e -> p i e", i=TILES)
         xn_dram = xn.rearrange("b h w c -> (b h w) c").rearrange("(p i) c -> p i c", i=TILES)
@@ -44,24 +48,25 @@ def tile_transformerconvblock_pb_kernel(
         w_dram = ffn1_w.rearrange("(n j r) c -> j n r c", n=CHUNKS, r=ROWS)
         wo_dram = W_O.rearrange("(u q e) c -> q u e c", u=2, e=2)
 
-        ident_f32 = keep.tile([P, P], F32)
-        masks.make_identity(nc, ident_f32[:])
-        ident_bf16 = keep.tile([P, P], BF16)
-        masks.make_identity(nc, ident_bf16[:])
-        ones = keep.tile([P, P], BF16)
-        nc.vector.memset(ones[:], 1.0)
         bias_row = keep.tile([P, F], BF16)
         nc.vector.memset(bias_row[:], 0.0)
+        nc.scalar.dma_start(out=bias_row[0:1, :], in_=ffn1_b.rearrange("(a f) -> a f", a=1))
         attn_bf16 = keep.tile([P, 1], BF16)
         ffn_bf16 = keep.tile([P, 1], BF16)
         with nc.allow_non_contiguous_dma(reason="one bfloat16 scalar to every partition"):
             nc.scalar.dma_start(out=attn_bf16[:], in_=scale_attn.partition_broadcast(P))
             nc.scalar.dma_start(out=ffn_bf16[:], in_=scale_ffn.partition_broadcast(P))
-        nc.scalar.dma_start(out=bias_row[0:1, :], in_=ffn1_b.rearrange("(a f) -> a f", a=1))
+        ident_f32 = keep.tile([P, P], F32)
+        nc.vector.memset(ident_f32[:], 0.0)
+        masks.make_identity(nc, ident_f32[:], nomemset=True)
+        ident_bf16 = keep.tile([P, P], BF16)
+        nc.vector.tensor_copy(out=ident_bf16[:], in_=ident_f32[:])
+        ones = keep.tile([P, P], BF16)
+        nc.vector.memset(ones[:], 1.0)
         attn = keep.tile([P, 1], F32)
-        nc.vector.tensor_copy(out=attn[:], in_=attn_bf16[:])
+        nc.gpsimd.tensor_copy(out=attn[:], in_=attn_bf16[:])
         ffn = keep.tile([P, 1], F32)
-        nc.vector.tensor_copy(out=ffn[:], in_=ffn_bf16[:])
+        nc.gpsimd.tensor_copy(out=ffn[:], in_=ffn_bf16[:])
 
         wo_raw = keep.tile([P, PACK * K], BF16)
         o_sb = keep.tile([P, TILES * K], BF16)
@@ -93,7 +98,7 @@ def tile_transformerconvblock_pb_kernel(
         y_codes = keep.tile([P, TOKENS], U32, align_bytes=64)
         y_scales = keep.tile([P, TOKENS], U8, align_bytes=64)
         z_sb = keep.tile([P, TILES * K], BF16)
-        bias_all = keep.tile([P, F], F32)
+        bias_all = keep.tile([P, F], BF16)
 
         def quantise(grouped, codes, scales, start, count):
             nc.vector.quantize_mx(
@@ -101,12 +106,6 @@ def tile_transformerconvblock_pb_kernel(
                 scales=scales[:, start : start + count],
                 in_=grouped[:, PACK * start : PACK * (start + count)],
             )
-
-        nc.vector.tensor_copy(
-            out=wo_grouped[:].rearrange("q (c t) -> q c t", t=PACK),
-            in_=wo_raw[:].rearrange("q (t c) -> q c t", t=PACK),
-        )
-        quantise(wo_grouped, wo_codes, wo_scales, 0, K)
 
         o_words = o_sb[:].bitcast(F32).rearrange("p (i u q) -> p i u q", i=TILES, u=2)
         o_grouped_words = o_grouped[:].bitcast(F32).rearrange("q (i p u) -> q i p u", i=TILES, u=2)
@@ -117,46 +116,53 @@ def tile_transformerconvblock_pb_kernel(
             "q (n j r u) -> q n j r u", n=CHUNKS, r=ROWS, u=2
         )
 
-        def prepare_o(half):
-            for i in range(half * HALF, (half + 1) * HALF, 2):
-                bank = psum_words.tile([P, 2, 2, P], F32, tag="words")
-                for a in range(2):
-                    for u in range(2):
-                        nc.tensor.transpose(bank[:, a, u, :], o_words[:, i + a, u, :], ident_f32[:])
-                nc.scalar.copy(
-                    out=o_grouped_words[:, i : i + 2, :, :],
-                    in_=bank[:].rearrange("q a u p -> q a p u"),
-                )
-            quantise(o_grouped, o_codes, o_scales, half * HALF * P, HALF * P)
+        def transpose_o(pair):
+            i = 2 * pair
+            bank = psum_words.tile([P, 2, 2, P], F32, tag="words")
+            for a in range(2):
+                for u in range(2):
+                    nc.tensor.transpose(bank[:, a, u, :], o_words[:, i + a, u, :], ident_f32[:])
+            nc.scalar.copy(
+                out=o_grouped_words[:, i : i + 2, :, :],
+                in_=bank[:].rearrange("q a u p -> q a p u"),
+            )
 
-        def prepare_w(n):
-            for r in range(0, ROWS, 2):
-                bank = psum_words.tile([P, 2, 2, P], F32, tag="words")
-                for a in range(2):
-                    for u in range(2):
-                        nc.tensor.transpose(bank[:, a, u, :], w_words[:, n, r + a, u, :], ident_f32[:])
-                nc.scalar.copy(
-                    out=w_grouped_words[:, n, :, r : r + 2, :],
-                    in_=bank[:].rearrange("q a u j -> q j a u"),
-                )
-            quantise(w_grouped, w_codes, w_scales, n * CHUNK, CHUNK)
+        def transpose_w(k):
+            n, r = k // 2, 2 * (k % 2)
+            bank = psum_words.tile([P, 2, 2, P], F32, tag="words")
+            for a in range(2):
+                for u in range(2):
+                    nc.tensor.transpose(bank[:, a, u, :], w_words[:, n, r + a, u, :], ident_f32[:])
+            copy = nc.vector.tensor_copy if n == 0 else nc.scalar.copy
+            copy(
+                out=w_grouped_words[:, n, :, r : r + 2, :],
+                in_=bank[:].rearrange("q a u j -> q j a u"),
+            )
 
-        def spread_bias():
-            for n in range(CHUNKS):
-                cols = slice(n * CHUNK, (n + 1) * CHUNK)
-                bank = psum_u.tile([P, CHUNK], F32, tag="u")
-                nc.tensor.matmul(out=bank[:], lhsT=ones[:], rhs=bias_row[:, cols], start=True, stop=True)
-                nc.scalar.copy(out=bias_all[:, cols], in_=bank[:])
+        def spread_bias(half):
+            b = half * 2 * CHUNK
+            bank = psum_u.tile([P, 2 * CHUNK], BF16, tag="u")
+            for c in range(0, 2 * CHUNK, CHUNK):
+                nc.tensor.matmul(
+                    out=bank[:, c : c + CHUNK],
+                    lhsT=ones[:],
+                    rhs=bias_row[:, b + c : b + c + CHUNK],
+                    start=True,
+                    stop=True,
+                )
+            nc.scalar.copy(out=bias_all[:, b : b + 2 * CHUNK], in_=bank[:])
 
         z_pairs = z_sb[:].rearrange("p (i u q e) -> p i u q e", i=TILES, u=2, e=2)
         y_grouped_tiles = y_grouped[:].rearrange("q (i p t) -> q i p t", i=TILES, t=PACK)
+        p_banks = {}
+        z_banks = {}
+        u_banks = {}
 
         def first_matmul(i):
             tokens = slice(i * P, (i + 1) * P)
-            cols = slice(i * K, (i + 1) * K)
-            p_bank = psum_p.tile([P, K], F32, tag="p")
+            p_banks[i] = psum_first.tile([P, K], F32, name="p_bank", tag="first")
             nc.tensor.matmul_mx(
-                out=p_bank[:],
+                out=p_banks[i][:],
                 lhsT=o_codes[:, tokens].bitcast(FP8X4),
                 lhsT_scale=o_scales[:, tokens],
                 rhs=wo_codes[:].bitcast(FP8X4),
@@ -164,67 +170,124 @@ def tile_transformerconvblock_pb_kernel(
                 start=True,
                 stop=True,
             )
+
+        def add_xn(i):
+            cols = slice(i * K, (i + 1) * K)
             nc.vector.scalar_tensor_tensor(
                 out=z_sb[:, cols],
-                in0=p_bank[:],
+                in0=p_banks[i][:],
                 scalar=attn[:, 0:1],
                 in1=xn_sb[:, cols],
                 op0=ALU.mult,
                 op1=ALU.add,
             )
-            z_bank = psum_z.tile([P, PACK, P], BF16, tag="z")
+
+        def transpose_z(i):
+            z_banks[i] = psum_first.tile([P, PACK, P], BF16, name="z_bank", tag="first")
             for u in range(2):
                 for e in range(2):
-                    nc.tensor.transpose(z_bank[:, 2 * u + e, :], z_pairs[:, i, u, :, e], ident_bf16[:])
+                    nc.tensor.transpose(
+                        z_banks[i][:, 2 * u + e, :], z_pairs[:, i, u, :, e], ident_bf16[:]
+                    )
+
+        def relu_z(i):
             nc.scalar.activation(
                 out=y_grouped_tiles[:, i, :, :],
-                in_=z_bank[:].rearrange("q t p -> q p t"),
+                in_=z_banks[i][:].rearrange("q t p -> q p t"),
                 func=ACT.Relu,
             )
-            quantise(y_grouped, y_codes, y_scales, i * P, P)
 
-        def second_matmul(i):
-            tokens = slice(i * P, (i + 1) * P)
-            h_tile = results.tile([P, F], F32, tag="h")
-            for n in range(CHUNKS):
-                cols = slice(n * CHUNK, (n + 1) * CHUNK)
-                u_bank = psum_u.tile([P, CHUNK], F32, tag="u")
-                nc.tensor.matmul_mx(
-                    out=u_bank[:],
-                    lhsT=y_codes[:, tokens].bitcast(FP8X4),
-                    lhsT_scale=y_scales[:, tokens],
-                    rhs=w_codes[:, cols].bitcast(FP8X4),
-                    rhs_scale=w_scales[:, cols],
-                    start=True,
-                    stop=True,
-                )
-                nc.vector.tensor_tensor(
-                    out=h_tile[:, cols], in0=u_bank[:], in1=bias_all[:, cols], op=ALU.add
-                )
-                if n % 2 == 0:
-                    nc.scalar.activation(
-                        out=h_tile[:, cols], in_=h_tile[:, cols], func=ACT.Relu, scale=ffn[:, 0:1]
-                    )
-                else:
-                    nc.gpsimd.tensor_scalar(
-                        out=h_tile[:, cols],
-                        in0=h_tile[:, cols],
-                        scalar1=ffn[:, 0:1],
-                        scalar2=0.0,
-                        op0=ALU.mult,
-                        op1=ALU.max,
-                    )
-            nc.sync.dma_start(out=out_dram[:, i, :], in_=h_tile[:])
+        def tile_and_chunk(b):
+            pair, rest = divmod(b, ROUND)
+            return 2 * pair + rest % 2, rest // 2
 
-        prepare_o(0)
-        for i in range(LEAD):
-            first_matmul(i)
-        spread_bias()
-        for n in range(CHUNKS):
-            prepare_w(n)
-        for i in range(LEAD, TILES + LEAD):
-            if i == HALF:
-                prepare_o(1)
-            if i < TILES:
-                first_matmul(i)
-            second_matmul(i - LEAD)
+        def second_matmul(b):
+            j, n = tile_and_chunk(b)
+            tokens = slice(j * P, (j + 1) * P)
+            cols = slice(n * CHUNK, (n + 1) * CHUNK)
+            u_banks[b] = psum_u.tile([P, CHUNK], F32, name="u_bank", tag="u")
+            nc.tensor.matmul_mx(
+                out=u_banks[b][:],
+                lhsT=y_codes[:, tokens].bitcast(FP8X4),
+                lhsT_scale=y_scales[:, tokens],
+                rhs=w_codes[:, cols].bitcast(FP8X4),
+                rhs_scale=w_scales[:, cols],
+                start=True,
+                stop=True,
+            )
+
+        def second_epilogue(b):
+            j, n = tile_and_chunk(b)
+            cols = slice(n * CHUNK, (n + 1) * CHUNK)
+            h_tile = results.tile([P, CHUNK], F32, tag="h")
+            nc.vector.tensor_tensor(out=h_tile[:], in0=u_banks[b][:], in1=bias_all[:, cols], op=ALU.add)
+            nc.scalar.activation(out=h_tile[:], in_=h_tile[:], func=ACT.Relu, scale=ffn[:, 0:1])
+            nc.sync.dma_start(out=out_dram[:, j, cols], in_=h_tile[:])
+
+        def quantise_o(pair):
+            quantise(o_grouped, o_codes, o_scales, 2 * pair * P, 2 * P)
+
+        def quantise_y(pair):
+            quantise(y_grouped, y_codes, y_scales, 2 * pair * P, 2 * P)
+
+        def quantise_w(n):
+            quantise(w_grouped, w_codes, w_scales, n * CHUNK, CHUNK)
+
+        nc.vector.tensor_copy(
+            out=wo_grouped[:].rearrange("q (c t) -> q c t", t=PACK),
+            in_=wo_raw[:].rearrange("q (t c) -> q c t", t=PACK),
+        )
+        quantise(wo_grouped, wo_codes, wo_scales, 0, K)
+        transpose_o(0)
+        quantise_o(0)
+        transpose_o(1)
+        spread_bias(0)
+        first_matmul(0)
+        first_matmul(1)
+        add_xn(0)
+        add_xn(1)
+        transpose_w(0)
+        transpose_w(1)
+        transpose_z(0)
+        transpose_z(1)
+        relu_z(0)
+        relu_z(1)
+        quantise_o(1)
+        quantise_w(0)
+        transpose_w(2)
+        transpose_w(3)
+        quantise_y(0)
+        spread_bias(1)
+
+        for s in range(BANKS + AHEAD):
+            this_pair, t = divmod(s, ROUND)
+            pair = this_pair + 1
+            a = 2 * pair
+            if s < BANKS:
+                second_matmul(s)
+            if s + 4 < W_BANKS:
+                transpose_w(s + 4)
+            if pair + 1 < PAIRS and t == 4:
+                transpose_o(pair + 1)
+            if pair < PAIRS and t == 0:
+                first_matmul(a)
+                first_matmul(a + 1)
+            if pair < PAIRS and t == 2:
+                transpose_z(a)
+            if pair < PAIRS and t == 3:
+                transpose_z(a + 1)
+                relu_z(a)
+            if pair < PAIRS and t == 4:
+                relu_z(a + 1)
+            if s >= AHEAD:
+                second_epilogue(s - AHEAD)
+            if s % 2 == 0 and s // 2 + 1 < CHUNKS:
+                quantise_w(s // 2 + 1)
+            if pair < PAIRS and t == 1:
+                add_xn(a)
+            if pair < PAIRS and t == 2:
+                add_xn(a + 1)
+            if pair < PAIRS and t == 7:
+                quantise_y(pair)
+            if pair + 1 < PAIRS and t == 7:
+                quantise_o(pair + 1)

@@ -35,7 +35,6 @@ def tile_transformerconvblock_pb_kernel(
 ):
     nc = tc.nc
     with ExitStack() as ctx:
-        ctx.enter_context(tc.manual_schedule())
         keep = ctx.enter_context(tc.tile_pool(name="keep", bufs=1))
         results = ctx.enter_context(tc.tile_pool(name="results", bufs=12))
         psum_words = ctx.enter_context(tc.psum_pool(name="psum_words", bufs=2))
@@ -49,25 +48,13 @@ def tile_transformerconvblock_pb_kernel(
         wo_dram = W_O.rearrange("(u q e) c -> q u e c", u=2, e=2)
 
         bias_row = keep.tile([P, F], BF16)
-        nc.vector.memset(bias_row[:], 0.0)
-        nc.scalar.dma_start(out=bias_row[0:1, :], in_=ffn1_b.rearrange("(a f) -> a f", a=1))
         attn_bf16 = keep.tile([P, 1], BF16)
         ffn_bf16 = keep.tile([P, 1], BF16)
-        with nc.allow_non_contiguous_dma(reason="one bfloat16 scalar to every partition"):
-            nc.scalar.dma_start(out=attn_bf16[:], in_=scale_attn.partition_broadcast(P))
-            nc.scalar.dma_start(out=ffn_bf16[:], in_=scale_ffn.partition_broadcast(P))
-        ident_f32 = keep.tile([P, P], F32)
-        nc.vector.memset(ident_f32[:], 0.0)
-        masks.make_identity(nc, ident_f32[:], nomemset=True)
-        ident_bf16 = keep.tile([P, P], BF16)
-        nc.vector.tensor_copy(out=ident_bf16[:], in_=ident_f32[:])
-        ones = keep.tile([P, P], BF16)
-        nc.vector.memset(ones[:], 1.0)
         attn = keep.tile([P, 1], F32)
-        nc.gpsimd.tensor_copy(out=attn[:], in_=attn_bf16[:])
         ffn = keep.tile([P, 1], F32)
-        nc.gpsimd.tensor_copy(out=ffn[:], in_=ffn_bf16[:])
-
+        ident_f32 = keep.tile([P, P], F32)
+        ident_bf16 = keep.tile([P, P], BF16)
+        ones = keep.tile([P, P], BF16)
         wo_raw = keep.tile([P, PACK * K], BF16)
         o_sb = keep.tile([P, TILES * K], BF16)
         xn_sb = keep.tile([P, TILES * K], BF16)
@@ -77,13 +64,6 @@ def tile_transformerconvblock_pb_kernel(
         w_chunks = w_sb[:].rearrange("j (n r c) -> j n r c", n=CHUNKS, r=ROWS)
         first = slice(0, HALF)
         second = slice(HALF, TILES)
-        nc.sync.dma_start(out=wo_raw[:].rearrange("q (u e c) -> q u e c", u=2, e=2), in_=wo_dram)
-        nc.sync.dma_start(out=o_tiles[:, first, :], in_=o_dram[:, first, :])
-        nc.sync.dma_start(out=xn_tiles[:, first, :], in_=xn_dram[:, first, :])
-        for n in range(CHUNKS):
-            nc.sync.dma_start(out=w_chunks[:, n], in_=w_dram[:, n])
-        nc.sync.dma_start(out=o_tiles[:, second, :], in_=o_dram[:, second, :])
-        nc.sync.dma_start(out=xn_tiles[:, second, :], in_=xn_dram[:, second, :])
 
         wo_grouped = keep.tile([P, K * PACK], BF16, align_bytes=64)
         wo_codes = keep.tile([P, K], U32, align_bytes=64)
@@ -233,31 +213,56 @@ def tile_transformerconvblock_pb_kernel(
         def quantise_w(n):
             quantise(w_grouped, w_codes, w_scales, n * CHUNK, CHUNK)
 
-        nc.vector.tensor_copy(
-            out=wo_grouped[:].rearrange("q (c t) -> q c t", t=PACK),
-            in_=wo_raw[:].rearrange("q (t c) -> q c t", t=PACK),
-        )
-        quantise(wo_grouped, wo_codes, wo_scales, 0, K)
-        transpose_o(0)
-        quantise_o(0)
-        transpose_o(1)
-        spread_bias(0)
-        first_matmul(0)
-        first_matmul(1)
-        add_xn(0)
-        add_xn(1)
-        transpose_w(0)
-        transpose_w(1)
-        transpose_z(0)
-        transpose_z(1)
-        relu_z(0)
-        relu_z(1)
-        quantise_o(1)
-        quantise_w(0)
-        transpose_w(2)
-        transpose_w(3)
-        quantise_y(0)
-        spread_bias(1)
+        def load_everything():
+            nc.vector.memset(bias_row[:], 0.0)
+            nc.scalar.dma_start(out=bias_row[0:1, :], in_=ffn1_b.rearrange("(a f) -> a f", a=1))
+            with nc.allow_non_contiguous_dma(reason="one bfloat16 scalar to every partition"):
+                nc.scalar.dma_start(out=attn_bf16[:], in_=scale_attn.partition_broadcast(P))
+                nc.scalar.dma_start(out=ffn_bf16[:], in_=scale_ffn.partition_broadcast(P))
+            nc.sync.dma_start(out=wo_raw[:].rearrange("q (u e c) -> q u e c", u=2, e=2), in_=wo_dram)
+            nc.sync.dma_start(out=o_tiles[:, first, :], in_=o_dram[:, first, :])
+            nc.sync.dma_start(out=xn_tiles[:, first, :], in_=xn_dram[:, first, :])
+            for n in range(CHUNKS):
+                nc.sync.dma_start(out=w_chunks[:, n], in_=w_dram[:, n])
+            nc.sync.dma_start(out=o_tiles[:, second, :], in_=o_dram[:, second, :])
+            nc.sync.dma_start(out=xn_tiles[:, second, :], in_=xn_dram[:, second, :])
+
+        def make_constants():
+            nc.vector.memset(ident_f32[:], 0.0)
+            masks.make_identity(nc, ident_f32[:], nomemset=True)
+            nc.vector.tensor_copy(out=ident_bf16[:], in_=ident_f32[:])
+            nc.vector.memset(ones[:], 1.0)
+            nc.gpsimd.tensor_copy(out=attn[:], in_=attn_bf16[:])
+            nc.gpsimd.tensor_copy(out=ffn[:], in_=ffn_bf16[:])
+
+        with tc.manual_schedule():
+            load_everything()
+            make_constants()
+            nc.vector.tensor_copy(
+                out=wo_grouped[:].rearrange("q (c t) -> q c t", t=PACK),
+                in_=wo_raw[:].rearrange("q (t c) -> q c t", t=PACK),
+            )
+            quantise(wo_grouped, wo_codes, wo_scales, 0, K)
+            transpose_o(0)
+            quantise_o(0)
+            transpose_o(1)
+            spread_bias(0)
+            first_matmul(0)
+            first_matmul(1)
+            add_xn(0)
+            add_xn(1)
+            transpose_w(0)
+            transpose_w(1)
+            transpose_z(0)
+            transpose_z(1)
+            relu_z(0)
+            relu_z(1)
+            quantise_o(1)
+            quantise_w(0)
+            transpose_w(2)
+            transpose_w(3)
+            quantise_y(0)
+            spread_bias(1)
 
         for s in range(BANKS + AHEAD):
             this_pair, t = divmod(s, ROUND)

@@ -17,15 +17,11 @@ TOKENS = 4 * 16 * 16
 K = 512
 F = 2048
 TILES = TOKENS // P
-HALF = TILES // 2
+PAIRS = TILES // 2
 CHUNK = 512
 CHUNKS = F // CHUNK
 ROWS = CHUNK // P
-PAIRS = TILES // 2
-ROUND = 2 * CHUNKS
-BANKS = PAIRS * ROUND
-W_BANKS = 2 * CHUNKS
-AHEAD = 2
+RESULT_TILES = 12
 
 FLOPS = 2 * TOKENS * K * K + 2 * TOKENS * K * F
 
@@ -36,10 +32,10 @@ def tile_transformerconvblock_pb_kernel(
     nc = tc.nc
     with ExitStack() as ctx:
         keep = ctx.enter_context(tc.tile_pool(name="keep", bufs=1))
-        results = ctx.enter_context(tc.tile_pool(name="results", bufs=12))
+        results = ctx.enter_context(tc.tile_pool(name="results", bufs=RESULT_TILES))
         psum_words = ctx.enter_context(tc.psum_pool(name="psum_words", bufs=2))
         psum_first = ctx.enter_context(tc.psum_pool(name="psum_first", bufs=3))
-        psum_u = ctx.enter_context(tc.psum_pool(name="psum_u", bufs=AHEAD + 1))
+        psum_second = ctx.enter_context(tc.psum_pool(name="psum_second", bufs=3))
 
         o_dram = o.rearrange("b h w e -> (b h w) e").rearrange("(p i) e -> p i e", i=TILES)
         xn_dram = xn.rearrange("b h w c -> (b h w) c").rearrange("(p i) c -> p i c", i=TILES)
@@ -62,8 +58,6 @@ def tile_transformerconvblock_pb_kernel(
         o_tiles = o_sb[:].rearrange("p (i e) -> p i e", i=TILES)
         xn_tiles = xn_sb[:].rearrange("p (i c) -> p i c", i=TILES)
         w_chunks = w_sb[:].rearrange("j (n r c) -> j n r c", n=CHUNKS, r=ROWS)
-        first = slice(0, HALF)
-        second = slice(HALF, TILES)
 
         wo_grouped = keep.tile([P, K * PACK], BF16, align_bytes=64)
         wo_codes = keep.tile([P, K], U32, align_bytes=64)
@@ -80,12 +74,51 @@ def tile_transformerconvblock_pb_kernel(
         z_sb = keep.tile([P, TILES * K], BF16)
         bias_all = keep.tile([P, F], BF16)
 
-        def quantise(grouped, codes, scales, start, count):
-            nc.vector.quantize_mx(
-                out=codes[:, start : start + count].bitcast(FP8X4),
-                scales=scales[:, start : start + count],
-                in_=grouped[:, PACK * start : PACK * (start + count)],
+        def load_everything():
+            nc.vector.memset(bias_row[:], 0.0)
+            with nc.allow_non_contiguous_dma(reason="one bfloat16 scalar to every partition"):
+                nc.scalar.dma_start(out=attn_bf16[:], in_=scale_attn.partition_broadcast(P))
+                nc.scalar.dma_start(
+                    out=bias_row[0:1, :], in_=ffn1_b.rearrange("(x f) -> x f", x=1)
+                )
+                nc.scalar.dma_start(out=ffn_bf16[:], in_=scale_ffn.partition_broadcast(P))
+            pair_0 = slice(0, 2)
+            pair_1 = slice(2, 4)
+            later_pairs = slice(4, TILES)
+            nc.sync.dma_start(
+                out=wo_raw[:].rearrange("q (u e c) -> q u e c", u=2, e=2), in_=wo_dram
             )
+            nc.sync.dma_start(out=o_tiles[:, pair_0, :], in_=o_dram[:, pair_0, :])
+            nc.sync.dma_start(out=xn_tiles[:, pair_0, :], in_=xn_dram[:, pair_0, :])
+            nc.sync.dma_start(out=o_tiles[:, pair_1, :], in_=o_dram[:, pair_1, :])
+            nc.sync.dma_start(out=w_chunks[:, 0], in_=w_dram[:, 0])
+            nc.sync.dma_start(out=xn_tiles[:, pair_1, :], in_=xn_dram[:, pair_1, :])
+            for n in range(1, CHUNKS):
+                nc.sync.dma_start(out=w_chunks[:, n], in_=w_dram[:, n])
+            nc.sync.dma_start(out=o_tiles[:, later_pairs, :], in_=o_dram[:, later_pairs, :])
+            nc.sync.dma_start(out=xn_tiles[:, later_pairs, :], in_=xn_dram[:, later_pairs, :])
+
+        def make_constants():
+            nc.vector.memset(ident_f32[:], 0.0)
+            masks.make_identity(nc, ident_f32[:], nomemset=True)
+            nc.vector.tensor_copy(out=ident_bf16[:], in_=ident_f32[:])
+            nc.vector.memset(ones[:], 1.0)
+            nc.gpsimd.tensor_copy(out=attn[:], in_=attn_bf16[:])
+            nc.gpsimd.tensor_copy(out=ffn[:], in_=ffn_bf16[:])
+
+        def quantise(grouped, codes, scales, first_col, count):
+            nc.vector.quantize_mx(
+                out=codes[:, first_col : first_col + count].bitcast(FP8X4),
+                scales=scales[:, first_col : first_col + count],
+                in_=grouped[:, PACK * first_col : PACK * (first_col + count)],
+            )
+
+        def quantise_wo():
+            nc.vector.tensor_copy(
+                out=wo_grouped[:].rearrange("q (c t) -> q c t", t=PACK),
+                in_=wo_raw[:].rearrange("q (t c) -> q c t", t=PACK),
+            )
+            quantise(wo_grouped, wo_codes, wo_scales, 0, K)
 
         o_words = o_sb[:].bitcast(F32).rearrange("p (i u q) -> p i u q", i=TILES, u=2)
         o_grouped_words = o_grouped[:].bitcast(F32).rearrange("q (i p u) -> q i p u", i=TILES, u=2)
@@ -107,8 +140,10 @@ def tile_transformerconvblock_pb_kernel(
                 in_=bank[:].rearrange("q a u p -> q a p u"),
             )
 
-        def transpose_w(k):
-            n, r = k // 2, 2 * (k % 2)
+        def quantise_o(pair):
+            quantise(o_grouped, o_codes, o_scales, 2 * pair * P, 2 * P)
+
+        def transpose_w(n, r):
             bank = psum_words.tile([P, 2, 2, P], F32, tag="words")
             for a in range(2):
                 for u in range(2):
@@ -119,24 +154,26 @@ def tile_transformerconvblock_pb_kernel(
                 in_=bank[:].rearrange("q a u j -> q j a u"),
             )
 
+        def quantise_w(n):
+            quantise(w_grouped, w_codes, w_scales, n * CHUNK, CHUNK)
+
         def spread_bias(half):
-            b = half * 2 * CHUNK
-            bank = psum_u.tile([P, 2 * CHUNK], BF16, tag="u")
-            for c in range(0, 2 * CHUNK, CHUNK):
+            first_col = half * 2 * CHUNK
+            bank = psum_second.tile([P, 2 * CHUNK], BF16, tag="second")
+            for col in range(0, 2 * CHUNK, CHUNK):
                 nc.tensor.matmul(
-                    out=bank[:, c : c + CHUNK],
+                    out=bank[:, col : col + CHUNK],
                     lhsT=ones[:],
-                    rhs=bias_row[:, b + c : b + c + CHUNK],
+                    rhs=bias_row[:, first_col + col : first_col + col + CHUNK],
                     start=True,
                     stop=True,
                 )
-            nc.scalar.copy(out=bias_all[:, b : b + 2 * CHUNK], in_=bank[:])
+            nc.scalar.copy(out=bias_all[:, first_col : first_col + 2 * CHUNK], in_=bank[:])
 
         z_pairs = z_sb[:].rearrange("p (i u q e) -> p i u q e", i=TILES, u=2, e=2)
         y_grouped_tiles = y_grouped[:].rearrange("q (i p t) -> q i p t", i=TILES, t=PACK)
         p_banks = {}
         z_banks = {}
-        u_banks = {}
 
         def first_matmul(i):
             tokens = slice(i * P, (i + 1) * P)
@@ -177,17 +214,15 @@ def tile_transformerconvblock_pb_kernel(
                 func=ACT.Relu,
             )
 
-        def tile_and_chunk(b):
-            pair, rest = divmod(b, ROUND)
-            return 2 * pair + rest % 2, rest // 2
+        def quantise_y(pair):
+            quantise(y_grouped, y_codes, y_scales, 2 * pair * P, 2 * P)
 
-        def second_matmul(b):
-            j, n = tile_and_chunk(b)
-            tokens = slice(j * P, (j + 1) * P)
+        def second_matmul(i, n):
+            tokens = slice(i * P, (i + 1) * P)
             cols = slice(n * CHUNK, (n + 1) * CHUNK)
-            u_banks[b] = psum_u.tile([P, CHUNK], F32, name="u_bank", tag="u")
+            u_bank = psum_second.tile([P, CHUNK], F32, tag="second")
             nc.tensor.matmul_mx(
-                out=u_banks[b][:],
+                out=u_bank[:],
                 lhsT=y_codes[:, tokens].bitcast(FP8X4),
                 lhsT_scale=y_scales[:, tokens],
                 rhs=w_codes[:, cols].bitcast(FP8X4),
@@ -195,54 +230,15 @@ def tile_transformerconvblock_pb_kernel(
                 start=True,
                 stop=True,
             )
-
-        def second_epilogue(b):
-            j, n = tile_and_chunk(b)
-            cols = slice(n * CHUNK, (n + 1) * CHUNK)
             h_tile = results.tile([P, CHUNK], F32, tag="h")
-            nc.vector.tensor_tensor(out=h_tile[:], in0=u_banks[b][:], in1=bias_all[:, cols], op=ALU.add)
+            nc.vector.tensor_tensor(out=h_tile[:], in0=u_bank[:], in1=bias_all[:, cols], op=ALU.add)
             nc.scalar.activation(out=h_tile[:], in_=h_tile[:], func=ACT.Relu, scale=ffn[:, 0:1])
-            nc.sync.dma_start(out=out_dram[:, j, cols], in_=h_tile[:])
-
-        def quantise_o(pair):
-            quantise(o_grouped, o_codes, o_scales, 2 * pair * P, 2 * P)
-
-        def quantise_y(pair):
-            quantise(y_grouped, y_codes, y_scales, 2 * pair * P, 2 * P)
-
-        def quantise_w(n):
-            quantise(w_grouped, w_codes, w_scales, n * CHUNK, CHUNK)
-
-        def load_everything():
-            nc.vector.memset(bias_row[:], 0.0)
-            nc.scalar.dma_start(out=bias_row[0:1, :], in_=ffn1_b.rearrange("(a f) -> a f", a=1))
-            with nc.allow_non_contiguous_dma(reason="one bfloat16 scalar to every partition"):
-                nc.scalar.dma_start(out=attn_bf16[:], in_=scale_attn.partition_broadcast(P))
-                nc.scalar.dma_start(out=ffn_bf16[:], in_=scale_ffn.partition_broadcast(P))
-            nc.sync.dma_start(out=wo_raw[:].rearrange("q (u e c) -> q u e c", u=2, e=2), in_=wo_dram)
-            nc.sync.dma_start(out=o_tiles[:, first, :], in_=o_dram[:, first, :])
-            nc.sync.dma_start(out=xn_tiles[:, first, :], in_=xn_dram[:, first, :])
-            for n in range(CHUNKS):
-                nc.sync.dma_start(out=w_chunks[:, n], in_=w_dram[:, n])
-            nc.sync.dma_start(out=o_tiles[:, second, :], in_=o_dram[:, second, :])
-            nc.sync.dma_start(out=xn_tiles[:, second, :], in_=xn_dram[:, second, :])
-
-        def make_constants():
-            nc.vector.memset(ident_f32[:], 0.0)
-            masks.make_identity(nc, ident_f32[:], nomemset=True)
-            nc.vector.tensor_copy(out=ident_bf16[:], in_=ident_f32[:])
-            nc.vector.memset(ones[:], 1.0)
-            nc.gpsimd.tensor_copy(out=attn[:], in_=attn_bf16[:])
-            nc.gpsimd.tensor_copy(out=ffn[:], in_=ffn_bf16[:])
+            nc.sync.dma_start(out=out_dram[:, i, cols], in_=h_tile[:])
 
         with tc.manual_schedule():
             load_everything()
             make_constants()
-            nc.vector.tensor_copy(
-                out=wo_grouped[:].rearrange("q (c t) -> q c t", t=PACK),
-                in_=wo_raw[:].rearrange("q (t c) -> q c t", t=PACK),
-            )
-            quantise(wo_grouped, wo_codes, wo_scales, 0, K)
+            quantise_wo()
             transpose_o(0)
             quantise_o(0)
             transpose_o(1)
@@ -251,48 +247,35 @@ def tile_transformerconvblock_pb_kernel(
             first_matmul(1)
             add_xn(0)
             add_xn(1)
-            transpose_w(0)
-            transpose_w(1)
+            transpose_w(0, 0)
+            transpose_w(0, 2)
             transpose_z(0)
             transpose_z(1)
             relu_z(0)
             relu_z(1)
             quantise_o(1)
             quantise_w(0)
-            transpose_w(2)
-            transpose_w(3)
+            transpose_w(1, 0)
+            transpose_w(1, 2)
             quantise_y(0)
             spread_bias(1)
+            quantise_w(1)
 
-        for s in range(BANKS + AHEAD):
-            this_pair, t = divmod(s, ROUND)
-            pair = this_pair + 1
-            a = 2 * pair
-            if s < BANKS:
-                second_matmul(s)
-            if s + 4 < W_BANKS:
-                transpose_w(s + 4)
-            if pair + 1 < PAIRS and t == 4:
-                transpose_o(pair + 1)
-            if pair < PAIRS and t == 0:
-                first_matmul(a)
-                first_matmul(a + 1)
-            if pair < PAIRS and t == 2:
-                transpose_z(a)
-            if pair < PAIRS and t == 3:
-                transpose_z(a + 1)
-                relu_z(a)
-            if pair < PAIRS and t == 4:
-                relu_z(a + 1)
-            if s >= AHEAD:
-                second_epilogue(s - AHEAD)
-            if s % 2 == 0 and s // 2 + 1 < CHUNKS:
-                quantise_w(s // 2 + 1)
-            if pair < PAIRS and t == 1:
-                add_xn(a)
-            if pair < PAIRS and t == 2:
-                add_xn(a + 1)
-            if pair < PAIRS and t == 7:
-                quantise_y(pair)
-            if pair + 1 < PAIRS and t == 7:
-                quantise_o(pair + 1)
+        for pair in range(PAIRS):
+            if pair + 1 < PAIRS:
+                for i in (2 * pair + 2, 2 * pair + 3):
+                    first_matmul(i)
+                    add_xn(i)
+                    transpose_z(i)
+                    relu_z(i)
+                quantise_y(pair + 1)
+            if pair + 2 < PAIRS:
+                transpose_o(pair + 2)
+                quantise_o(pair + 2)
+            for n in range(CHUNKS):
+                for i in (2 * pair, 2 * pair + 1):
+                    second_matmul(i, n)
+                if pair == 0 and n + 2 < CHUNKS:
+                    transpose_w(n + 2, 0)
+                    transpose_w(n + 2, 2)
+                    quantise_w(n + 2)

from contextlib import ExitStack

import concourse.masks as masks
import concourse.mybir as mybir

F32 = mybir.dt.float32
BF16 = mybir.dt.bfloat16
U32 = mybir.dt.uint32
U8 = mybir.dt.uint8
FP8X4 = mybir.dt.float8_e4m3fn_x4
ALU = mybir.AluOpType
ACT = mybir.ActivationFunctionType

P = 128
PACK = 4
TOKENS = 4 * 16 * 16
K = 512
F = 2048
TILES = TOKENS // P
PAIRS = TILES // 2
CHUNK = 512
CHUNKS = F // CHUNK
ROWS = CHUNK // P
RESULT_TILES = 12

FLOPS = 2 * TOKENS * K * K + 2 * TOKENS * K * F


def tile_transformerconvblock_pb_kernel(
    tc, o, xn, W_O, scale_attn, ffn1_w, ffn1_b, scale_ffn, out
):
    nc = tc.nc
    with ExitStack() as ctx:
        keep = ctx.enter_context(tc.tile_pool(name="keep", bufs=1))
        results = ctx.enter_context(tc.tile_pool(name="results", bufs=RESULT_TILES))
        psum_words = ctx.enter_context(tc.psum_pool(name="psum_words", bufs=2))
        psum_first = ctx.enter_context(tc.psum_pool(name="psum_first", bufs=3))
        psum_second = ctx.enter_context(tc.psum_pool(name="psum_second", bufs=3))

        o_dram = o.rearrange("b h w e -> (b h w) e").rearrange("(p i) e -> p i e", i=TILES)
        xn_dram = xn.rearrange("b h w c -> (b h w) c").rearrange("(p i) c -> p i c", i=TILES)
        out_dram = out.rearrange("b h w f -> (b h w) f").rearrange("(p i) f -> p i f", i=TILES)
        w_dram = ffn1_w.rearrange("(n j r) c -> j n r c", n=CHUNKS, r=ROWS)
        wo_dram = W_O.rearrange("(u q e) c -> q u e c", u=2, e=2)

        bias_row = keep.tile([P, F], BF16)
        attn_bf16 = keep.tile([P, 1], BF16)
        ffn_bf16 = keep.tile([P, 1], BF16)
        attn = keep.tile([P, 1], F32)
        ffn = keep.tile([P, 1], F32)
        ident_f32 = keep.tile([P, P], F32)
        ident_bf16 = keep.tile([P, P], BF16)
        ones = keep.tile([P, P], BF16)
        wo_raw = keep.tile([P, PACK * K], BF16)
        o_sb = keep.tile([P, TILES * K], BF16)
        xn_sb = keep.tile([P, TILES * K], BF16)
        w_sb = keep.tile([P, CHUNKS * ROWS * K], BF16)
        o_tiles = o_sb[:].rearrange("p (i e) -> p i e", i=TILES)
        xn_tiles = xn_sb[:].rearrange("p (i c) -> p i c", i=TILES)
        w_chunks = w_sb[:].rearrange("j (n r c) -> j n r c", n=CHUNKS, r=ROWS)

        wo_grouped = keep.tile([P, K * PACK], BF16, align_bytes=64)
        wo_codes = keep.tile([P, K], U32, align_bytes=64)
        wo_scales = keep.tile([P, K], U8, align_bytes=64)
        o_grouped = keep.tile([P, TOKENS * PACK], BF16, align_bytes=64)
        o_codes = keep.tile([P, TOKENS], U32, align_bytes=64)
        o_scales = keep.tile([P, TOKENS], U8, align_bytes=64)
        w_grouped = keep.tile([P, F * PACK], BF16, align_bytes=64)
        w_codes = keep.tile([P, F], U32, align_bytes=64)
        w_scales = keep.tile([P, F], U8, align_bytes=64)
        y_grouped = keep.tile([P, TOKENS * PACK], BF16, align_bytes=64)
        y_codes = keep.tile([P, TOKENS], U32, align_bytes=64)
        y_scales = keep.tile([P, TOKENS], U8, align_bytes=64)
        z_sb = keep.tile([P, TILES * K], BF16)
        bias_all = keep.tile([P, F], BF16)

        def load_everything():
            nc.vector.memset(bias_row[:], 0.0)
            with nc.allow_non_contiguous_dma(reason="one bfloat16 scalar to every partition"):
                nc.scalar.dma_start(out=attn_bf16[:], in_=scale_attn.partition_broadcast(P))
                nc.scalar.dma_start(
                    out=bias_row[0:1, :], in_=ffn1_b.rearrange("(x f) -> x f", x=1)
                )
                nc.scalar.dma_start(out=ffn_bf16[:], in_=scale_ffn.partition_broadcast(P))
            pair_0 = slice(0, 2)
            pair_1 = slice(2, 4)
            later_pairs = slice(4, TILES)
            nc.sync.dma_start(
                out=wo_raw[:].rearrange("q (u e c) -> q u e c", u=2, e=2), in_=wo_dram
            )
            nc.sync.dma_start(out=o_tiles[:, pair_0, :], in_=o_dram[:, pair_0, :])
            nc.sync.dma_start(out=xn_tiles[:, pair_0, :], in_=xn_dram[:, pair_0, :])
            nc.sync.dma_start(out=o_tiles[:, pair_1, :], in_=o_dram[:, pair_1, :])
            nc.sync.dma_start(out=w_chunks[:, 0], in_=w_dram[:, 0])
            nc.sync.dma_start(out=xn_tiles[:, pair_1, :], in_=xn_dram[:, pair_1, :])
            for n in range(1, CHUNKS):
                nc.sync.dma_start(out=w_chunks[:, n], in_=w_dram[:, n])
            nc.sync.dma_start(out=o_tiles[:, later_pairs, :], in_=o_dram[:, later_pairs, :])
            nc.sync.dma_start(out=xn_tiles[:, later_pairs, :], in_=xn_dram[:, later_pairs, :])

        def make_constants():
            nc.vector.memset(ident_f32[:], 0.0)
            masks.make_identity(nc, ident_f32[:], nomemset=True)
            nc.vector.tensor_copy(out=ident_bf16[:], in_=ident_f32[:])
            nc.vector.memset(ones[:], 1.0)
            nc.gpsimd.tensor_copy(out=attn[:], in_=attn_bf16[:])
            nc.gpsimd.tensor_copy(out=ffn[:], in_=ffn_bf16[:])

        def quantise(grouped, codes, scales, first_col, count):
            nc.vector.quantize_mx(
                out=codes[:, first_col : first_col + count].bitcast(FP8X4),
                scales=scales[:, first_col : first_col + count],
                in_=grouped[:, PACK * first_col : PACK * (first_col + count)],
            )

        def quantise_wo():
            nc.vector.tensor_copy(
                out=wo_grouped[:].rearrange("q (c t) -> q c t", t=PACK),
                in_=wo_raw[:].rearrange("q (t c) -> q c t", t=PACK),
            )
            quantise(wo_grouped, wo_codes, wo_scales, 0, K)

        o_words = o_sb[:].bitcast(F32).rearrange("p (i u q) -> p i u q", i=TILES, u=2)
        o_grouped_words = o_grouped[:].bitcast(F32).rearrange("q (i p u) -> q i p u", i=TILES, u=2)
        w_words = w_sb[:].bitcast(F32).rearrange(
            "j (n r u q) -> j n r u q", n=CHUNKS, r=ROWS, u=2
        )
        w_grouped_words = w_grouped[:].bitcast(F32).rearrange(
            "q (n j r u) -> q n j r u", n=CHUNKS, r=ROWS, u=2
        )

        def transpose_o(pair):
            i = 2 * pair
            bank = psum_words.tile([P, 2, 2, P], F32, tag="words")
            for a in range(2):
                for u in range(2):
                    nc.tensor.transpose(bank[:, a, u, :], o_words[:, i + a, u, :], ident_f32[:])
            nc.scalar.copy(
                out=o_grouped_words[:, i : i + 2, :, :],
                in_=bank[:].rearrange("q a u p -> q a p u"),
            )

        def quantise_o(pair):
            quantise(o_grouped, o_codes, o_scales, 2 * pair * P, 2 * P)

        def transpose_w(n, r):
            bank = psum_words.tile([P, 2, 2, P], F32, tag="words")
            for a in range(2):
                for u in range(2):
                    nc.tensor.transpose(bank[:, a, u, :], w_words[:, n, r + a, u, :], ident_f32[:])
            copy = nc.vector.tensor_copy if n == 0 else nc.scalar.copy
            copy(
                out=w_grouped_words[:, n, :, r : r + 2, :],
                in_=bank[:].rearrange("q a u j -> q j a u"),
            )

        def quantise_w(n):
            quantise(w_grouped, w_codes, w_scales, n * CHUNK, CHUNK)

        def spread_bias(half):
            first_col = half * 2 * CHUNK
            bank = psum_second.tile([P, 2 * CHUNK], BF16, tag="second")
            for col in range(0, 2 * CHUNK, CHUNK):
                nc.tensor.matmul(
                    out=bank[:, col : col + CHUNK],
                    lhsT=ones[:],
                    rhs=bias_row[:, first_col + col : first_col + col + CHUNK],
                    start=True,
                    stop=True,
                )
            nc.scalar.copy(out=bias_all[:, first_col : first_col + 2 * CHUNK], in_=bank[:])

        z_pairs = z_sb[:].rearrange("p (i u q e) -> p i u q e", i=TILES, u=2, e=2)
        y_grouped_tiles = y_grouped[:].rearrange("q (i p t) -> q i p t", i=TILES, t=PACK)
        p_banks = {}
        z_banks = {}

        def first_matmul(i):
            tokens = slice(i * P, (i + 1) * P)
            p_banks[i] = psum_first.tile([P, K], F32, name="p_bank", tag="first")
            nc.tensor.matmul_mx(
                out=p_banks[i][:],
                lhsT=o_codes[:, tokens].bitcast(FP8X4),
                lhsT_scale=o_scales[:, tokens],
                rhs=wo_codes[:].bitcast(FP8X4),
                rhs_scale=wo_scales[:],
                start=True,
                stop=True,
            )

        def add_xn(i):
            cols = slice(i * K, (i + 1) * K)
            nc.vector.scalar_tensor_tensor(
                out=z_sb[:, cols],
                in0=p_banks[i][:],
                scalar=attn[:, 0:1],
                in1=xn_sb[:, cols],
                op0=ALU.mult,
                op1=ALU.add,
            )

        def transpose_z(i):
            z_banks[i] = psum_first.tile([P, PACK, P], BF16, name="z_bank", tag="first")
            for u in range(2):
                for e in range(2):
                    nc.tensor.transpose(
                        z_banks[i][:, 2 * u + e, :], z_pairs[:, i, u, :, e], ident_bf16[:]
                    )

        def relu_z(i):
            nc.scalar.activation(
                out=y_grouped_tiles[:, i, :, :],
                in_=z_banks[i][:].rearrange("q t p -> q p t"),
                func=ACT.Relu,
            )

        def quantise_y(pair):
            quantise(y_grouped, y_codes, y_scales, 2 * pair * P, 2 * P)

        def second_matmul(i, n):
            tokens = slice(i * P, (i + 1) * P)
            cols = slice(n * CHUNK, (n + 1) * CHUNK)
            u_bank = psum_second.tile([P, CHUNK], F32, tag="second")
            nc.tensor.matmul_mx(
                out=u_bank[:],
                lhsT=y_codes[:, tokens].bitcast(FP8X4),
                lhsT_scale=y_scales[:, tokens],
                rhs=w_codes[:, cols].bitcast(FP8X4),
                rhs_scale=w_scales[:, cols],
                start=True,
                stop=True,
            )
            h_tile = results.tile([P, CHUNK], F32, tag="h")
            nc.vector.tensor_tensor(out=h_tile[:], in0=u_bank[:], in1=bias_all[:, cols], op=ALU.add)
            nc.scalar.activation(out=h_tile[:], in_=h_tile[:], func=ACT.Relu, scale=ffn[:, 0:1])
            nc.sync.dma_start(out=out_dram[:, i, cols], in_=h_tile[:])

        with tc.manual_schedule():
            load_everything()
            make_constants()
            quantise_wo()
            transpose_o(0)
            quantise_o(0)
            transpose_o(1)
            spread_bias(0)
            first_matmul(0)
            first_matmul(1)
            add_xn(0)
            add_xn(1)
            transpose_w(0, 0)
            transpose_w(0, 2)
            transpose_z(0)
            transpose_z(1)
            relu_z(0)
            relu_z(1)
            quantise_o(1)
            quantise_w(0)
            transpose_w(1, 0)
            transpose_w(1, 2)
            quantise_y(0)
            spread_bias(1)
            quantise_w(1)

        for pair in range(PAIRS):
            if pair + 1 < PAIRS:
                for i in (2 * pair + 2, 2 * pair + 3):
                    first_matmul(i)
                    add_xn(i)
                    transpose_z(i)
                    relu_z(i)
                quantise_y(pair + 1)
            if pair + 2 < PAIRS:
                transpose_o(pair + 2)
                quantise_o(pair + 2)
            for n in range(CHUNKS):
                for i in (2 * pair, 2 * pair + 1):
                    second_matmul(i, n)
                if pair == 0 and n + 2 < CHUNKS:
                    transpose_w(n + 2, 0)
                    transpose_w(n + 2, 2)
                    quantise_w(n + 2)
